import numpy as np
import ml_dtypes


def mxq(x, axis, fmt="e4m3"):
    dtype, down = {"e4m3": (ml_dtypes.float8_e4m3fn, 7), "e5m2": (ml_dtypes.float8_e5m2, 14)}[fmt]
    v = np.moveaxis(np.asarray(x, np.float32).astype(ml_dtypes.bfloat16).astype(np.float64), axis, -1)
    blocks = v.reshape(v.shape[:-1] + (-1, 32))
    amax = np.abs(blocks).max(-1, keepdims=True)
    byte = np.maximum(np.where(amax > 0, np.frexp(amax)[1] - 1 + 127, 0) - down, 1)
    scale = np.exp2(byte - 127.0)
    codes = (blocks / scale).astype(np.float32).astype(dtype).astype(np.float64)
    return np.moveaxis((codes * scale).reshape(v.shape), -1, axis)


WIDE = False


def mx_kscale(k):
    if not WIDE:
        return np.ones(k)
    levels = np.array([10, -10, 5, -5, 0])
    a = np.random.permutation(np.resize(levels, k // 512 * 4)).reshape(k // 512, 4)
    idx = np.arange(k)
    return np.exp2(a[idx // 512, idx % 128 // 32])


BF16 = ml_dtypes.bfloat16


def bf(x):
    return np.asarray(x, np.float32).astype(BF16)


def f64(x):
    return np.asarray(x).astype(np.float64)


B, S, D, E = 2, 2048, 512, 256
EPS = 1e-5


def layer_norm(x, g, b):
    mu = x.mean(-1, keepdims=True)
    var = np.square(x - mu).mean(-1, keepdims=True)
    return (x - mu) / np.sqrt(var + EPS) * g + b


def setup_inputs():
    s = mx_kscale(D)

    def stream():
        return bf(np.random.standard_normal((B, S, D)) + 0.5 * np.random.standard_normal((B, S, 1)))

    def gain():
        return bf((1.0 + 0.1 * np.random.standard_normal(D)) * s)

    def shift():
        return bf(0.1 * np.random.standard_normal(D) * s)

    def weight(a):
        return bf(np.random.standard_normal((E, D)) * a / np.sqrt(D) / s[None, :])

    def bias():
        return bf(0.2 * np.random.standard_normal(E))

    return {"text": stream(), "img": stream(),
            "ln_t_g": gain(), "ln_t_b": shift(), "ln_i_g": gain(), "ln_i_b": shift(),
            "Wq": weight(1.5), "bq": bias(),
            "Wkt": weight(1.5), "bkt": bias(), "Wvt": weight(1.0), "bvt": bias(),
            "Wki": weight(1.5), "bki": bias(), "Wvi": weight(1.0), "bvi": bias()}


def reference(text, img, ln_t_g, ln_t_b, ln_i_g, ln_i_b, Wq, bq, Wkt, bkt, Wvt, bvt, Wki, bki, Wvi, bvi):
    tn = mxq(layer_norm(f64(text), f64(ln_t_g), f64(ln_t_b)), 2, "e4m3")
    im = mxq(layer_norm(f64(img), f64(ln_i_g), f64(ln_i_b)), 2, "e4m3")
    wq = mxq(f64(Wq), 1, "e4m3").T
    q = np.concatenate([(tn @ wq), (im @ wq)], 0) + f64(bq)
    k = np.concatenate([(tn @ mxq(f64(Wkt), 1, "e4m3").T) + f64(bkt), (im @ mxq(f64(Wki), 1, "e4m3").T) + f64(bki)], 0)
    v = np.concatenate([(tn @ mxq(f64(Wvt), 1, "e4m3").T) + f64(bvt), (im @ mxq(f64(Wvi), 1, "e4m3").T) + f64(bvi)], 0)
    return q, k, v

@@ -1,0 +1,276 @@
+from contextlib import ExitStack
+
+import concourse.mybir as mybir
+from concourse.masks import make_identity
+
+F32 = mybir.dt.float32
+BF16 = mybir.dt.bfloat16
+U32 = mybir.dt.uint32
+U8 = mybir.dt.uint8
+FP8X4 = mybir.dt.float8_e4m3fn_x4
+ACT = mybir.ActivationFunctionType
+ALU = mybir.AluOpType
+
+P = 128
+PACK = 4
+D = P * PACK
+E = 256
+SLOTS = 4
+GROUP = P * SLOTS
+TOKENS = 4096
+GROUPS_PER_STREAM = TOKENS // GROUP
+N_GROUPS = 2 * GROUPS_PER_STREAM
+N_WEIGHTS = 5
+BANK = 512
+EPS = 1e-5
+
+FLOPS = 2 * (2 * TOKENS) * D * (3 * E)
+
+LOADS_AHEAD = 2
+LAG_SCALARS = 1
+LAG_NORMALISE = 2
+LAG_TRANSPOSE = 3
+LAG_PROJECT = 4
+
+
+def tile_modalityadaptivemodule_pa_t_kernel(
+    tc,
+    text, img, ln_t_g, ln_t_b, ln_i_g, ln_i_b,
+    Wq, bq, Wkt, bkt, Wvt, bvt, Wki, bki, Wvi, bvi,
+    out_0, out_1, out_2,
+):
+    nc = tc.nc
+    weights = [Wq, Wkt, Wvt, Wki, Wvi]
+    biases = [bq, bkt, bvt, bki, bvi]
+    ln_vectors = [ln_t_g, ln_t_b, ln_i_g, ln_i_b]
+
+    def weight_index(stream, o):
+        return 0 if o == 0 else o + 2 * stream
+
+    x_groups = [
+        s.flatten_outer_dims().rearrange("(g p j) d -> g p (j d)", p=P, j=SLOTS) for s in (text, img)
+    ]
+    out_groups = [
+        o.flatten_outer_dims().rearrange("(g p j) e -> g p (j e)", p=P, j=SLOTS)
+        for o in (out_0, out_1, out_2)
+    ]
+
+    with ExitStack() as stack:
+        const = stack.enter_context(tc.tile_pool(name="const", bufs=1))
+        wprep = stack.enter_context(tc.tile_pool(name="wprep", bufs=2))
+        xs = stack.enter_context(tc.tile_pool(name="xs", bufs=LOADS_AHEAD + LAG_NORMALISE + 1))
+        small = stack.enter_context(tc.tile_pool(name="small", bufs=4))
+        work = stack.enter_context(tc.tile_pool(name="work", bufs=3))
+        banks_t = stack.enter_context(tc.psum_pool(name="banks_t", bufs=1))
+        banks_acc = stack.enter_context(tc.psum_pool(name="banks_acc", bufs=4))
+        stack.enter_context(tc.manual_schedule())
+
+        x_of, mean_var_of, neg_mean_of, rstd_of, xhat_of, grouped_of = {}, {}, {}, {}, {}, {}
+        w_rows_of, w_grouped_of = {}, {}
+
+        def load_group(g):
+            x = xs.tile([P, SLOTS, D], BF16, name="x")
+            nc.sync.dma_start(
+                out=x[:].rearrange("p j d -> p (j d)"),
+                in_=x_groups[g // GROUPS_PER_STREAM][g % GROUPS_PER_STREAM],
+            )
+            x_of[g] = x
+
+        for g in range(LOADS_AHEAD):
+            load_group(g)
+
+        ident_f32 = const.tile([P, P], F32, name="ident_f32")
+        make_identity(nc, ident_f32[:])
+        ident_bf16 = const.tile([P, P], BF16, name="ident_bf16")
+        make_identity(nc, ident_bf16[:])
+        eps = const.tile([P, 1], F32, name="eps")
+        nc.vector.memset(eps[:], EPS)
+
+        ln_rows = const.tile([P, P], BF16, name="ln_rows")
+        nc.vector.memset(ln_rows[:], 0.0)
+        for v, vector in enumerate(ln_vectors):
+            nc.sync.dma_start(
+                out=ln_rows[PACK * v : PACK * (v + 1), :], in_=vector.rearrange("(t c) -> t c", c=P)
+            )
+        ln_rows_t = banks_acc.tile([P, P], BF16, name="ln_rows_t", tag="acc")
+        nc.tensor.transpose(out=ln_rows_t[:], in_=ln_rows[:], identity=ident_bf16[:])
+        ln_cols = const.tile([P, PACK * len(ln_vectors)], F32, name="ln_cols")
+        nc.scalar.copy(out=ln_cols[:], in_=ln_rows_t[:, 0 : PACK * len(ln_vectors)])
+
+        bias_rows = const.tile([P, N_WEIGHTS * E], BF16, name="bias_rows")
+        nc.vector.memset(bias_rows[:], 0.0)
+        for w, bias in enumerate(biases):
+            nc.sync.dma_start(
+                out=bias_rows[0:1, w * E : (w + 1) * E], in_=bias.rearrange("(o e) -> o e", o=1)
+            )
+        ones = const.tile([P, P], BF16, name="ones")
+        nc.vector.memset(ones[:], 1.0)
+        bias_all = const.tile([P, N_WEIGHTS * E], F32, name="bias_all")
+        for c0 in range(0, N_WEIGHTS * E, BANK):
+            width = min(BANK, N_WEIGHTS * E - c0)
+            spread = banks_acc.tile([P, BANK], F32, name="spread", tag="acc")
+            nc.tensor.matmul(
+                out=spread[:, 0:width], lhsT=ones[:], rhs=bias_rows[:, c0 : c0 + width],
+                start=True, stop=True,
+            )
+            nc.scalar.copy(out=bias_all[:, c0 : c0 + width], in_=spread[:, 0:width])
+
+        w_codes = const.tile([P, N_WEIGHTS * E], U32, name="w_codes", align_bytes=64)
+        w_scales = const.tile([P, N_WEIGHTS * E], U8, name="w_scales", align_bytes=64)
+
+        def load_weight(w):
+            w_rows = wprep.tile([P, E // P, D], BF16, name="w_rows")
+            nc.sync.dma_start(out=w_rows[:], in_=weights[w].rearrange("(c p) k -> p c k", p=P))
+            w_rows_of[w] = w_rows
+
+        def transpose_weight(w):
+            w_grouped = wprep.tile([P, E, PACK], BF16, name="w_grouped", align_bytes=64)
+            for c in range(E // P):
+                w_t = banks_acc.tile([P, PACK, P], BF16, name="w_t", tag="acc")
+                for t in range(PACK):
+                    nc.tensor.transpose(
+                        out=w_t[:, t, :], in_=w_rows_of[w][:, c, t * P : (t + 1) * P],
+                        identity=ident_bf16[:],
+                    )
+                nc.scalar.copy(
+                    out=w_grouped[:, c * P : (c + 1) * P, :], in_=w_t[:].rearrange("p t e -> p e t")
+                )
+            w_grouped_of[w] = w_grouped
+
+        def quantise_weight(w):
+            nc.vector.quantize_mx(
+                out=w_codes[:, w * E : (w + 1) * E].bitcast(FP8X4),
+                scales=w_scales[:, w * E : (w + 1) * E],
+                in_=w_grouped_of[w][:].rearrange("p e t -> p (e t)"),
+            )
+
+        def statistics(g):
+            halves = small.tile([P, SLOTS, 6], F32, name="halves")
+            mean_var = small.tile([P, SLOTS, 2], F32, name="mean_var")
+            for j in range(SLOTS):
+                nc.vector.bn_stats(out=halves[:, j, :], in_=x_of[g][:, j, :])
+            for j in range(SLOTS):
+                nc.vector.bn_aggr(out=mean_var[:, j, :], in_=halves[:, j, :])
+            mean_var_of[g] = mean_var
+
+        def standard_deviation(g):
+            std = small.tile([P, SLOTS], F32, name="std")
+            nc.scalar.activation(
+                out=std[:], in_=mean_var_of[g][:, :, 1], func=ACT.Sqrt, bias=eps[:, 0:1], scale=1.0
+            )
+            return std
+
+        def negate_mean(g):
+            neg_mean = small.tile([P, SLOTS], F32, name="neg_mean")
+            nc.gpsimd.tensor_scalar(
+                out=neg_mean[:], in0=mean_var_of[g][:, :, 0], scalar1=-1.0, scalar2=0.0,
+                op0=ALU.mult, op1=ALU.add,
+            )
+            neg_mean_of[g] = neg_mean
+
+        def invert(g, std):
+            rstd = small.tile([P, SLOTS], F32, name="rstd")
+            nc.vector.reciprocal(out=rstd[:], in_=std[:])
+            rstd_of[g] = rstd
+
+        def normalise(g):
+            xhat = work.tile([P, SLOTS, D], F32, name="xhat")
+            for j in range(SLOTS):
+                nc.gpsimd.tensor_scalar(
+                    out=xhat[:, j, :], in0=x_of[g][:, j, :],
+                    scalar1=neg_mean_of[g][:, j : j + 1], scalar2=rstd_of[g][:, j : j + 1],
+                    op0=ALU.add, op1=ALU.mult,
+                )
+            xhat_of[g] = xhat
+
+        def transpose_group(g):
+            xhat_t = []
+            for t in range(PACK):
+                bank = banks_t.tile([P, GROUP], F32, name="xhat_t%d" % t)
+                for j in range(SLOTS):
+                    nc.tensor.transpose(
+                        out=bank[:, j * P : (j + 1) * P],
+                        in_=xhat_of[g][:, j, t * P : (t + 1) * P],
+                        identity=ident_f32[:],
+                    )
+                xhat_t.append(bank)
+            return xhat_t
+
+        def gain_shift_group(g, xhat_t):
+            first = 2 * PACK * (g // GROUPS_PER_STREAM)
+            planes = work.tile([P, PACK, GROUP], BF16, name="planes")
+            for t in range(PACK):
+                nc.scalar.activation(
+                    out=planes[:, t, :], in_=xhat_t[t][:], func=ACT.Identity,
+                    scale=ln_cols[:, first + t : first + t + 1],
+                    bias=ln_cols[:, first + PACK + t : first + PACK + t + 1],
+                )
+            grouped = work.tile([P, GROUP, PACK], BF16, name="grouped", align_bytes=64)
+            nc.scalar.copy(
+                out=grouped[:].rearrange("p (c i) t -> p c t i", i=4),
+                in_=planes[:].rearrange("p t (c i) -> p c t i", i=4),
+            )
+            grouped_of[g] = grouped
+
+        def quantise_group(g):
+            codes = work.tile([P, GROUP], U32, name="codes", align_bytes=64)
+            scales = work.tile([P, GROUP], U8, name="scales", align_bytes=64)
+            nc.vector.quantize_mx(
+                out=codes[:].bitcast(FP8X4), scales=scales[:],
+                in_=grouped_of[g][:].rearrange("p c t -> p (c t)"),
+            )
+            return codes, scales
+
+        def project_group(g, codes, scales):
+            stream = g // GROUPS_PER_STREAM
+            result = work.tile([P, 3, SLOTS, E], F32, name="result")
+            for j0 in range(0, SLOTS, 2):
+                for o in range(3):
+                    w_cols = slice(weight_index(stream, o) * E, (weight_index(stream, o) + 1) * E)
+                    acc = banks_acc.tile([P, 2, E], F32, name="acc", tag="acc")
+                    for jj in range(2):
+                        tokens = slice((j0 + jj) * P, (j0 + jj + 1) * P)
+                        nc.tensor.matmul_mx(
+                            out=acc[:, jj, :],
+                            lhsT=codes[:, tokens].bitcast(FP8X4), lhsT_scale=scales[:, tokens],
+                            rhs=w_codes[:, w_cols].bitcast(FP8X4), rhs_scale=w_scales[:, w_cols],
+                            start=True, stop=True,
+                        )
+                    nc.vector.tensor_tensor(
+                        out=result[:, o, j0 : j0 + 2, :], in0=acc[:],
+                        in1=bias_all[:, w_cols].unsqueeze(1).to_broadcast([P, 2, E]), op=ALU.add,
+                    )
+            for o in range(3):
+                nc.sync.dma_start(
+                    out=out_groups[o][g], in_=result[:, o, :, :].rearrange("p j e -> p (j e)")
+                )
+
+        def in_range(g):
+            return 0 <= g < N_GROUPS
+
+        for i in range(N_GROUPS + LAG_PROJECT):
+            if in_range(i + LOADS_AHEAD):
+                load_group(i + LOADS_AHEAD)
+            if i < N_WEIGHTS:
+                load_weight(i)
+            if in_range(i - LAG_PROJECT):
+                codes, scales = quantise_group(i - LAG_PROJECT)
+            if in_range(i - LAG_TRANSPOSE):
+                xhat_t = transpose_group(i - LAG_TRANSPOSE)
+            if 0 <= i - 1 < N_WEIGHTS:
+                transpose_weight(i - 1)
+            if in_range(i - LAG_SCALARS):
+                std = standard_deviation(i - LAG_SCALARS)
+                negate_mean(i - LAG_SCALARS)
+            if in_range(i - LAG_NORMALISE):
+                normalise(i - LAG_NORMALISE)
+            if in_range(i - LAG_TRANSPOSE):
+                gain_shift_group(i - LAG_TRANSPOSE, xhat_t)
+            if in_range(i):
+                statistics(i)
+            if in_range(i - LAG_SCALARS):
+                invert(i - LAG_SCALARS, std)
+            if 0 <= i - 1 < N_WEIGHTS:
+                quantise_weight(i - 1)
+            if in_range(i - LAG_PROJECT):
+                project_group(i - LAG_PROJECT, codes, scales)

@@ -31,6 +31,7 @@ LAG_SCALARS = 1
 LAG_NORMALISE = 2
 LAG_TRANSPOSE = 3
 LAG_PROJECT = 4
+LAG_V_BIAS = 5
 
 
 def tile_modalityadaptivemodule_pa_t_kernel(
@@ -44,8 +45,9 @@ def tile_modalityadaptivemodule_pa_t_kernel(
     biases = [bq, bkt, bvt, bki, bvi]
     ln_vectors = [ln_t_g, ln_t_b, ln_i_g, ln_i_b]
 
-    def weight_index(stream, o):
-        return 0 if o == 0 else o + 2 * stream
+    def weight_columns(g, o):
+        w = 0 if o == 0 else o + 2 * (g // GROUPS_PER_STREAM)
+        return slice(w * E, (w + 1) * E)
 
     x_groups = [
         s.flatten_outer_dims().rearrange("(g p j) d -> g p (j d)", p=P, j=SLOTS) for s in (text, img)
@@ -66,6 +68,7 @@ def tile_modalityadaptivemodule_pa_t_kernel(
         stack.enter_context(tc.manual_schedule())
 
         x_of, mean_var_of, neg_mean_of, rstd_of, xhat_of, grouped_of = {}, {}, {}, {}, {}, {}
+        result_v_of = {}
         w_rows_of, w_grouped_of = {}, {}
 
         def load_group(g):
@@ -222,11 +225,11 @@ def tile_modalityadaptivemodule_pa_t_kernel(
             return codes, scales
 
         def project_group(g, codes, scales):
-            stream = g // GROUPS_PER_STREAM
-            result = work.tile([P, 3, SLOTS, E], F32, name="result")
+            result_qk = work.tile([P, 2, SLOTS, E], F32, name="result_qk")
+            result_v = work.tile([P, SLOTS, E], F32, name="result_v")
             for j0 in range(0, SLOTS, 2):
                 for o in range(3):
-                    w_cols = slice(weight_index(stream, o) * E, (weight_index(stream, o) + 1) * E)
+                    w_cols = weight_columns(g, o)
                     acc = banks_acc.tile([P, 2, E], F32, name="acc", tag="acc")
                     for jj in range(2):
                         tokens = slice((j0 + jj) * P, (j0 + jj + 1) * P)
@@ -236,19 +239,33 @@ def tile_modalityadaptivemodule_pa_t_kernel(
                             rhs=w_codes[:, w_cols].bitcast(FP8X4), rhs_scale=w_scales[:, w_cols],
                             start=True, stop=True,
                         )
-                    nc.vector.tensor_tensor(
-                        out=result[:, o, j0 : j0 + 2, :], in0=acc[:],
-                        in1=bias_all[:, w_cols].unsqueeze(1).to_broadcast([P, 2, E]), op=ALU.add,
-                    )
-            for o in range(3):
+                    if o < 2:
+                        nc.vector.tensor_tensor(
+                            out=result_qk[:, o, j0 : j0 + 2, :], in0=acc[:],
+                            in1=bias_all[:, w_cols].unsqueeze(1).to_broadcast([P, 2, E]), op=ALU.add,
+                        )
+                    else:
+                        nc.scalar.copy(out=result_v[:, j0 : j0 + 2, :], in_=acc[:])
+            for o in range(2):
                 nc.sync.dma_start(
-                    out=out_groups[o][g], in_=result[:, o, :, :].rearrange("p j e -> p (j e)")
+                    out=out_groups[o][g], in_=result_qk[:, o, :, :].rearrange("p j e -> p (j e)")
                 )
+            result_v_of[g] = result_v
+
+        def add_v_bias(g):
+            nc.gpsimd.tensor_tensor(
+                out=result_v_of[g][:], in0=result_v_of[g][:],
+                in1=bias_all[:, weight_columns(g, 2)].unsqueeze(1).to_broadcast([P, SLOTS, E]),
+                op=ALU.add,
+            )
+            nc.sync.dma_start(
+                out=out_groups[2][g], in_=result_v_of[g][:].rearrange("p j e -> p (j e)")
+            )
 
         def in_range(g):
             return 0 <= g < N_GROUPS
 
-        for i in range(N_GROUPS + LAG_PROJECT):
+        for i in range(N_GROUPS + LAG_V_BIAS):
             if in_range(i + LOADS_AHEAD):
                 load_group(i + LOADS_AHEAD)
             if i < N_WEIGHTS:
@@ -262,6 +279,8 @@ def tile_modalityadaptivemodule_pa_t_kernel(
             if in_range(i - LAG_SCALARS):
                 std = standard_deviation(i - LAG_SCALARS)
                 negate_mean(i - LAG_SCALARS)
+            if in_range(i - LAG_V_BIAS):
+                add_v_bias(i - LAG_V_BIAS)
             if in_range(i - LAG_NORMALISE):
                 normalise(i - LAG_NORMALISE)
             if in_range(i - LAG_TRANSPOSE):

@@ -31,7 +31,6 @@ LAG_SCALARS = 1
 LAG_NORMALISE = 2
 LAG_TRANSPOSE = 3
 LAG_PROJECT = 4
-LAG_V_BIAS = 5
 
 
 def tile_modalityadaptivemodule_pa_t_kernel(
@@ -68,7 +67,6 @@ def tile_modalityadaptivemodule_pa_t_kernel(
         stack.enter_context(tc.manual_schedule())
 
         x_of, mean_var_of, neg_mean_of, rstd_of, xhat_of, grouped_of = {}, {}, {}, {}, {}, {}
-        result_v_of = {}
         w_rows_of, w_grouped_of = {}, {}
 
         def load_group(g):
@@ -163,6 +161,11 @@ def tile_modalityadaptivemodule_pa_t_kernel(
             )
             return std
 
+        def invert(g, std):
+            rstd = small.tile([P, SLOTS], F32, name="rstd")
+            nc.vector.reciprocal(out=rstd[:], in_=std[:])
+            rstd_of[g] = rstd
+
         def negate_mean(g):
             neg_mean = small.tile([P, SLOTS], F32, name="neg_mean")
             nc.gpsimd.tensor_scalar(
@@ -170,11 +173,6 @@ def tile_modalityadaptivemodule_pa_t_kernel(
                 op0=ALU.mult, op1=ALU.add,
             )
             neg_mean_of[g] = neg_mean
-
-        def invert(g, std):
-            rstd = small.tile([P, SLOTS], F32, name="rstd")
-            nc.vector.reciprocal(out=rstd[:], in_=std[:])
-            rstd_of[g] = rstd
 
         def normalise(g):
             xhat = work.tile([P, SLOTS, D], F32, name="xhat")
@@ -225,11 +223,12 @@ def tile_modalityadaptivemodule_pa_t_kernel(
             return codes, scales
 
         def project_group(g, codes, scales):
-            result_qk = work.tile([P, 2, SLOTS, E], F32, name="result_qk")
-            result_v = work.tile([P, SLOTS, E], F32, name="result_v")
+            result = work.tile([P, 3, SLOTS, E], F32, name="result")
             for j0 in range(0, SLOTS, 2):
                 for o in range(3):
                     w_cols = weight_columns(g, o)
+                    bias_twice = bias_all[:, w_cols].unsqueeze(1).to_broadcast([P, 2, E])
+                    last_bank = o == 2 and j0 == SLOTS - 2
                     acc = banks_acc.tile([P, 2, E], F32, name="acc", tag="acc")
                     for jj in range(2):
                         tokens = slice((j0 + jj) * P, (j0 + jj + 1) * P)
@@ -239,33 +238,23 @@ def tile_modalityadaptivemodule_pa_t_kernel(
                             rhs=w_codes[:, w_cols].bitcast(FP8X4), rhs_scale=w_scales[:, w_cols],
                             start=True, stop=True,
                         )
-                    if o < 2:
-                        nc.vector.tensor_tensor(
-                            out=result_qk[:, o, j0 : j0 + 2, :], in0=acc[:],
-                            in1=bias_all[:, w_cols].unsqueeze(1).to_broadcast([P, 2, E]), op=ALU.add,
+                    two_slots = result[:, o, j0 : j0 + 2, :]
+                    if last_bank:
+                        nc.scalar.copy(out=two_slots, in_=acc[:])
+                        nc.gpsimd.tensor_tensor(
+                            out=two_slots, in0=two_slots, in1=bias_twice, op=ALU.add
                         )
                     else:
-                        nc.scalar.copy(out=result_v[:, j0 : j0 + 2, :], in_=acc[:])
-            for o in range(2):
+                        nc.vector.tensor_tensor(out=two_slots, in0=acc[:], in1=bias_twice, op=ALU.add)
+            for o in range(3):
                 nc.sync.dma_start(
-                    out=out_groups[o][g], in_=result_qk[:, o, :, :].rearrange("p j e -> p (j e)")
+                    out=out_groups[o][g], in_=result[:, o, :, :].rearrange("p j e -> p (j e)")
                 )
-            result_v_of[g] = result_v
-
-        def add_v_bias(g):
-            nc.gpsimd.tensor_tensor(
-                out=result_v_of[g][:], in0=result_v_of[g][:],
-                in1=bias_all[:, weight_columns(g, 2)].unsqueeze(1).to_broadcast([P, SLOTS, E]),
-                op=ALU.add,
-            )
-            nc.sync.dma_start(
-                out=out_groups[2][g], in_=result_v_of[g][:].rearrange("p j e -> p (j e)")
-            )
 
         def in_range(g):
             return 0 <= g < N_GROUPS
 
-        for i in range(N_GROUPS + LAG_V_BIAS):
+        for i in range(N_GROUPS + LAG_PROJECT):
             if in_range(i + LOADS_AHEAD):
                 load_group(i + LOADS_AHEAD)
             if i < N_WEIGHTS:
@@ -279,8 +268,6 @@ def tile_modalityadaptivemodule_pa_t_kernel(
             if in_range(i - LAG_SCALARS):
                 std = standard_deviation(i - LAG_SCALARS)
                 negate_mean(i - LAG_SCALARS)
-            if in_range(i - LAG_V_BIAS):
-                add_v_bias(i - LAG_V_BIAS)
             if in_range(i - LAG_NORMALISE):
                 normalise(i - LAG_NORMALISE)
             if in_range(i - LAG_TRANSPOSE):

@@ -64,7 +64,6 @@ def tile_modalityadaptivemodule_pa_t_kernel(
         work = stack.enter_context(tc.tile_pool(name="work", bufs=3))
         banks_t = stack.enter_context(tc.psum_pool(name="banks_t", bufs=1))
         banks_acc = stack.enter_context(tc.psum_pool(name="banks_acc", bufs=4))
-        stack.enter_context(tc.manual_schedule())
 
         x_of, mean_var_of, neg_mean_of, rstd_of, xhat_of, grouped_of = {}, {}, {}, {}, {}, {}
         w_rows_of, w_grouped_of = {}, {}

@@ -26,11 +26,11 @@ EPS = 1e-5
 
 FLOPS = 2 * (2 * TOKENS) * D * (3 * E)
 
-LOADS_AHEAD = 2
+FIRST_LOADS = 2
 LAG_SCALARS = 1
 LAG_NORMALISE = 2
 LAG_TRANSPOSE = 3
-LAG_PROJECT = 4
+LAG_PROJECT = 5
 
 
 def tile_modalityadaptivemodule_pa_t_kernel(
@@ -59,10 +59,10 @@ def tile_modalityadaptivemodule_pa_t_kernel(
     with ExitStack() as stack:
         const = stack.enter_context(tc.tile_pool(name="const", bufs=1))
         wprep = stack.enter_context(tc.tile_pool(name="wprep", bufs=2))
-        xs = stack.enter_context(tc.tile_pool(name="xs", bufs=LOADS_AHEAD + LAG_NORMALISE + 1))
-        small = stack.enter_context(tc.tile_pool(name="small", bufs=4))
-        work = stack.enter_context(tc.tile_pool(name="work", bufs=3))
-        banks_t = stack.enter_context(tc.psum_pool(name="banks_t", bufs=1))
+        xs = stack.enter_context(tc.tile_pool(name="xs", bufs=N_GROUPS))
+        small = stack.enter_context(tc.tile_pool(name="small", bufs=6))
+        work = stack.enter_context(tc.tile_pool(name="work", bufs=4))
+        banks_t = stack.enter_context(tc.psum_pool(name="banks_t", bufs=2))
         banks_acc = stack.enter_context(tc.psum_pool(name="banks_acc", bufs=4))
 
         x_of, mean_var_of, neg_mean_of, rstd_of, xhat_of, grouped_of = {}, {}, {}, {}, {}, {}
@@ -76,7 +76,7 @@ def tile_modalityadaptivemodule_pa_t_kernel(
             )
             x_of[g] = x
 
-        for g in range(LOADS_AHEAD):
+        for g in range(FIRST_LOADS):
             load_group(g)
 
         ident_f32 = const.tile([P, P], F32, name="ident_f32")
@@ -119,7 +119,7 @@ def tile_modalityadaptivemodule_pa_t_kernel(
         w_scales = const.tile([P, N_WEIGHTS * E], U8, name="w_scales", align_bytes=64)
 
         def load_weight(w):
-            w_rows = wprep.tile([P, E // P, D], BF16, name="w_rows")
+            w_rows = wprep.tile([P, E // P, D], BF16, name="w_rows", bufs=N_WEIGHTS)
             nc.sync.dma_start(out=w_rows[:], in_=weights[w].rearrange("(c p) k -> p c k", p=P))
             w_rows_of[w] = w_rows
 
@@ -185,15 +185,16 @@ def tile_modalityadaptivemodule_pa_t_kernel(
 
         def transpose_group(g):
             xhat_t = []
-            for t in range(PACK):
-                bank = banks_t.tile([P, GROUP], F32, name="xhat_t%d" % t)
-                for j in range(SLOTS):
-                    nc.tensor.transpose(
-                        out=bank[:, j * P : (j + 1) * P],
-                        in_=xhat_of[g][:, j, t * P : (t + 1) * P],
-                        identity=ident_f32[:],
-                    )
-                xhat_t.append(bank)
+            for t0 in range(0, PACK, 2):
+                two_banks = banks_t.tile([P, 2, GROUP], F32, name="two_banks")
+                for t in range(t0, t0 + 2):
+                    for j in range(SLOTS):
+                        nc.tensor.transpose(
+                            out=two_banks[:, t - t0, j * P : (j + 1) * P],
+                            in_=xhat_of[g][:, j, t * P : (t + 1) * P],
+                            identity=ident_f32[:],
+                        )
+                    xhat_t.append(two_banks[:, t - t0, :])
             return xhat_t
 
         def gain_shift_group(g, xhat_t):
@@ -201,7 +202,7 @@ def tile_modalityadaptivemodule_pa_t_kernel(
             planes = work.tile([P, PACK, GROUP], BF16, name="planes")
             for t in range(PACK):
                 nc.scalar.activation(
-                    out=planes[:, t, :], in_=xhat_t[t][:], func=ACT.Identity,
+                    out=planes[:, t, :], in_=xhat_t[t], func=ACT.Identity,
                     scale=ln_cols[:, first + t : first + t + 1],
                     bias=ln_cols[:, first + PACK + t : first + PACK + t + 1],
                 )
@@ -253,11 +254,12 @@ def tile_modalityadaptivemodule_pa_t_kernel(
         def in_range(g):
             return 0 <= g < N_GROUPS
 
+        for w in range(N_WEIGHTS):
+            load_weight(w)
+        for g in range(FIRST_LOADS, N_GROUPS):
+            load_group(g)
+
         for i in range(N_GROUPS + LAG_PROJECT):
-            if in_range(i + LOADS_AHEAD):
-                load_group(i + LOADS_AHEAD)
-            if i < N_WEIGHTS:
-                load_weight(i)
             if in_range(i - LAG_PROJECT):
                 codes, scales = quantise_group(i - LAG_PROJECT)
             if in_range(i - LAG_TRANSPOSE):

@@ -32,6 +32,8 @@ LAG_NORMALISE = 2
 LAG_TRANSPOSE = 3
 LAG_PROJECT = 5
 
+VECTOR_COLUMNS = 96
+
 
 def tile_modalityadaptivemodule_pa_t_kernel(
     tc,
@@ -207,9 +209,13 @@ def tile_modalityadaptivemodule_pa_t_kernel(
                     bias=ln_cols[:, first + PACK + t : first + PACK + t + 1],
                 )
             grouped = work.tile([P, GROUP, PACK], BF16, name="grouped", align_bytes=64)
+            nc.vector.tensor_copy(
+                out=grouped[:, :VECTOR_COLUMNS, :].rearrange("p (c i) t -> p c t i", i=4),
+                in_=planes[:, :, :VECTOR_COLUMNS].rearrange("p t (c i) -> p c t i", i=4),
+            )
             nc.scalar.copy(
-                out=grouped[:].rearrange("p (c i) t -> p c t i", i=4),
-                in_=planes[:].rearrange("p t (c i) -> p c t i", i=4),
+                out=grouped[:, VECTOR_COLUMNS:, :].rearrange("p (c i) t -> p c t i", i=4),
+                in_=planes[:, :, VECTOR_COLUMNS:].rearrange("p t (c i) -> p c t i", i=4),
             )
             grouped_of[g] = grouped
 

from contextlib import ExitStack

import concourse.mybir as mybir
from concourse.masks import make_identity

F32 = mybir.dt.float32
BF16 = mybir.dt.bfloat16
U32 = mybir.dt.uint32
U8 = mybir.dt.uint8
FP8X4 = mybir.dt.float8_e4m3fn_x4
ACT = mybir.ActivationFunctionType
ALU = mybir.AluOpType

P = 128
PACK = 4
D = P * PACK
E = 256
SLOTS = 4
GROUP = P * SLOTS
TOKENS = 4096
GROUPS_PER_STREAM = TOKENS // GROUP
N_GROUPS = 2 * GROUPS_PER_STREAM
N_WEIGHTS = 5
BANK = 512
EPS = 1e-5

FLOPS = 2 * (2 * TOKENS) * D * (3 * E)

FIRST_LOADS = 2
LAG_SCALARS = 1
LAG_NORMALISE = 2
LAG_TRANSPOSE = 3
LAG_PROJECT = 5

VECTOR_COLUMNS = 96


def tile_modalityadaptivemodule_pa_t_kernel(
    tc,
    text, img, ln_t_g, ln_t_b, ln_i_g, ln_i_b,
    Wq, bq, Wkt, bkt, Wvt, bvt, Wki, bki, Wvi, bvi,
    out_0, out_1, out_2,
):
    nc = tc.nc
    weights = [Wq, Wkt, Wvt, Wki, Wvi]
    biases = [bq, bkt, bvt, bki, bvi]
    ln_vectors = [ln_t_g, ln_t_b, ln_i_g, ln_i_b]

    def weight_columns(g, o):
        w = 0 if o == 0 else o + 2 * (g // GROUPS_PER_STREAM)
        return slice(w * E, (w + 1) * E)

    x_groups = [
        s.flatten_outer_dims().rearrange("(g p j) d -> g p (j d)", p=P, j=SLOTS) for s in (text, img)
    ]
    out_groups = [
        o.flatten_outer_dims().rearrange("(g p j) e -> g p (j e)", p=P, j=SLOTS)
        for o in (out_0, out_1, out_2)
    ]

    with ExitStack() as stack:
        const = stack.enter_context(tc.tile_pool(name="const", bufs=1))
        wprep = stack.enter_context(tc.tile_pool(name="wprep", bufs=2))
        xs = stack.enter_context(tc.tile_pool(name="xs", bufs=N_GROUPS))
        small = stack.enter_context(tc.tile_pool(name="small", bufs=6))
        work = stack.enter_context(tc.tile_pool(name="work", bufs=4))
        banks_t = stack.enter_context(tc.psum_pool(name="banks_t", bufs=2))
        banks_acc = stack.enter_context(tc.psum_pool(name="banks_acc", bufs=4))

        x_of, mean_var_of, neg_mean_of, rstd_of, xhat_of, grouped_of = {}, {}, {}, {}, {}, {}
        w_rows_of, w_grouped_of = {}, {}

        def load_group(g):
            x = xs.tile([P, SLOTS, D], BF16, name="x")
            nc.sync.dma_start(
                out=x[:].rearrange("p j d -> p (j d)"),
                in_=x_groups[g // GROUPS_PER_STREAM][g % GROUPS_PER_STREAM],
            )
            x_of[g] = x

        for g in range(FIRST_LOADS):
            load_group(g)

        ident_f32 = const.tile([P, P], F32, name="ident_f32")
        make_identity(nc, ident_f32[:])
        ident_bf16 = const.tile([P, P], BF16, name="ident_bf16")
        make_identity(nc, ident_bf16[:])
        eps = const.tile([P, 1], F32, name="eps")
        nc.vector.memset(eps[:], EPS)

        ln_rows = const.tile([P, P], BF16, name="ln_rows")
        nc.vector.memset(ln_rows[:], 0.0)
        for v, vector in enumerate(ln_vectors):
            nc.sync.dma_start(
                out=ln_rows[PACK * v : PACK * (v + 1), :], in_=vector.rearrange("(t c) -> t c", c=P)
            )
        ln_rows_t = banks_acc.tile([P, P], BF16, name="ln_rows_t", tag="acc")
        nc.tensor.transpose(out=ln_rows_t[:], in_=ln_rows[:], identity=ident_bf16[:])
        ln_cols = const.tile([P, PACK * len(ln_vectors)], F32, name="ln_cols")
        nc.scalar.copy(out=ln_cols[:], in_=ln_rows_t[:, 0 : PACK * len(ln_vectors)])

        bias_rows = const.tile([P, N_WEIGHTS * E], BF16, name="bias_rows")
        nc.vector.memset(bias_rows[:], 0.0)
        for w, bias in enumerate(biases):
            nc.sync.dma_start(
                out=bias_rows[0:1, w * E : (w + 1) * E], in_=bias.rearrange("(o e) -> o e", o=1)
            )
        ones = const.tile([P, P], BF16, name="ones")
        nc.vector.memset(ones[:], 1.0)
        bias_all = const.tile([P, N_WEIGHTS * E], F32, name="bias_all")
        for c0 in range(0, N_WEIGHTS * E, BANK):
            width = min(BANK, N_WEIGHTS * E - c0)
            spread = banks_acc.tile([P, BANK], F32, name="spread", tag="acc")
            nc.tensor.matmul(
                out=spread[:, 0:width], lhsT=ones[:], rhs=bias_rows[:, c0 : c0 + width],
                start=True, stop=True,
            )
            nc.scalar.copy(out=bias_all[:, c0 : c0 + width], in_=spread[:, 0:width])

        w_codes = const.tile([P, N_WEIGHTS * E], U32, name="w_codes", align_bytes=64)
        w_scales = const.tile([P, N_WEIGHTS * E], U8, name="w_scales", align_bytes=64)

        def load_weight(w):
            w_rows = wprep.tile([P, E // P, D], BF16, name="w_rows", bufs=N_WEIGHTS)
            nc.sync.dma_start(out=w_rows[:], in_=weights[w].rearrange("(c p) k -> p c k", p=P))
            w_rows_of[w] = w_rows

        def transpose_weight(w):
            w_grouped = wprep.tile([P, E, PACK], BF16, name="w_grouped", align_bytes=64)
            for c in range(E // P):
                w_t = banks_acc.tile([P, PACK, P], BF16, name="w_t", tag="acc")
                for t in range(PACK):
                    nc.tensor.transpose(
                        out=w_t[:, t, :], in_=w_rows_of[w][:, c, t * P : (t + 1) * P],
                        identity=ident_bf16[:],
                    )
                nc.scalar.copy(
                    out=w_grouped[:, c * P : (c + 1) * P, :], in_=w_t[:].rearrange("p t e -> p e t")
                )
            w_grouped_of[w] = w_grouped

        def quantise_weight(w):
            nc.vector.quantize_mx(
                out=w_codes[:, w * E : (w + 1) * E].bitcast(FP8X4),
                scales=w_scales[:, w * E : (w + 1) * E],
                in_=w_grouped_of[w][:].rearrange("p e t -> p (e t)"),
            )

        def statistics(g):
            halves = small.tile([P, SLOTS, 6], F32, name="halves")
            mean_var = small.tile([P, SLOTS, 2], F32, name="mean_var")
            for j in range(SLOTS):
                nc.vector.bn_stats(out=halves[:, j, :], in_=x_of[g][:, j, :])
            for j in range(SLOTS):
                nc.vector.bn_aggr(out=mean_var[:, j, :], in_=halves[:, j, :])
            mean_var_of[g] = mean_var

        def standard_deviation(g):
            std = small.tile([P, SLOTS], F32, name="std")
            nc.scalar.activation(
                out=std[:], in_=mean_var_of[g][:, :, 1], func=ACT.Sqrt, bias=eps[:, 0:1], scale=1.0
            )
            return std

        def invert(g, std):
            rstd = small.tile([P, SLOTS], F32, name="rstd")
            nc.vector.reciprocal(out=rstd[:], in_=std[:])
            rstd_of[g] = rstd

        def negate_mean(g):
            neg_mean = small.tile([P, SLOTS], F32, name="neg_mean")
            nc.gpsimd.tensor_scalar(
                out=neg_mean[:], in0=mean_var_of[g][:, :, 0], scalar1=-1.0, scalar2=0.0,
                op0=ALU.mult, op1=ALU.add,
            )
            neg_mean_of[g] = neg_mean

        def normalise(g):
            xhat = work.tile([P, SLOTS, D], F32, name="xhat")
            for j in range(SLOTS):
                nc.gpsimd.tensor_scalar(
                    out=xhat[:, j, :], in0=x_of[g][:, j, :],
                    scalar1=neg_mean_of[g][:, j : j + 1], scalar2=rstd_of[g][:, j : j + 1],
                    op0=ALU.add, op1=ALU.mult,
                )
            xhat_of[g] = xhat

        def transpose_group(g):
            xhat_t = []
            for t0 in range(0, PACK, 2):
                two_banks = banks_t.tile([P, 2, GROUP], F32, name="two_banks")
                for t in range(t0, t0 + 2):
                    for j in range(SLOTS):
                        nc.tensor.transpose(
                            out=two_banks[:, t - t0, j * P : (j + 1) * P],
                            in_=xhat_of[g][:, j, t * P : (t + 1) * P],
                            identity=ident_f32[:],
                        )
                    xhat_t.append(two_banks[:, t - t0, :])
            return xhat_t

        def gain_shift_group(g, xhat_t):
            first = 2 * PACK * (g // GROUPS_PER_STREAM)
            planes = work.tile([P, PACK, GROUP], BF16, name="planes")
            for t in range(PACK):
                nc.scalar.activation(
                    out=planes[:, t, :], in_=xhat_t[t], func=ACT.Identity,
                    scale=ln_cols[:, first + t : first + t + 1],
                    bias=ln_cols[:, first + PACK + t : first + PACK + t + 1],
                )
            grouped = work.tile([P, GROUP, PACK], BF16, name="grouped", align_bytes=64)
            nc.vector.tensor_copy(
                out=grouped[:, :VECTOR_COLUMNS, :].rearrange("p (c i) t -> p c t i", i=4),
                in_=planes[:, :, :VECTOR_COLUMNS].rearrange("p t (c i) -> p c t i", i=4),
            )
            nc.scalar.copy(
                out=grouped[:, VECTOR_COLUMNS:, :].rearrange("p (c i) t -> p c t i", i=4),
                in_=planes[:, :, VECTOR_COLUMNS:].rearrange("p t (c i) -> p c t i", i=4),
            )
            grouped_of[g] = grouped

        def quantise_group(g):
            codes = work.tile([P, GROUP], U32, name="codes", align_bytes=64)
            scales = work.tile([P, GROUP], U8, name="scales", align_bytes=64)
            nc.vector.quantize_mx(
                out=codes[:].bitcast(FP8X4), scales=scales[:],
                in_=grouped_of[g][:].rearrange("p c t -> p (c t)"),
            )
            return codes, scales

        def project_group(g, codes, scales):
            result = work.tile([P, 3, SLOTS, E], F32, name="result")
            for j0 in range(0, SLOTS, 2):
                for o in range(3):
                    w_cols = weight_columns(g, o)
                    bias_twice = bias_all[:, w_cols].unsqueeze(1).to_broadcast([P, 2, E])
                    last_bank = o == 2 and j0 == SLOTS - 2
                    acc = banks_acc.tile([P, 2, E], F32, name="acc", tag="acc")
                    for jj in range(2):
                        tokens = slice((j0 + jj) * P, (j0 + jj + 1) * P)
                        nc.tensor.matmul_mx(
                            out=acc[:, jj, :],
                            lhsT=codes[:, tokens].bitcast(FP8X4), lhsT_scale=scales[:, tokens],
                            rhs=w_codes[:, w_cols].bitcast(FP8X4), rhs_scale=w_scales[:, w_cols],
                            start=True, stop=True,
                        )
                    two_slots = result[:, o, j0 : j0 + 2, :]
                    if last_bank:
                        nc.scalar.copy(out=two_slots, in_=acc[:])
                        nc.gpsimd.tensor_tensor(
                            out=two_slots, in0=two_slots, in1=bias_twice, op=ALU.add
                        )
                    else:
                        nc.vector.tensor_tensor(out=two_slots, in0=acc[:], in1=bias_twice, op=ALU.add)
            for o in range(3):
                nc.sync.dma_start(
                    out=out_groups[o][g], in_=result[:, o, :, :].rearrange("p j e -> p (j e)")
                )

        def in_range(g):
            return 0 <= g < N_GROUPS

        for w in range(N_WEIGHTS):
            load_weight(w)
        for g in range(FIRST_LOADS, N_GROUPS):
            load_group(g)

        for i in range(N_GROUPS + LAG_PROJECT):
            if in_range(i - LAG_PROJECT):
                codes, scales = quantise_group(i - LAG_PROJECT)
            if in_range(i - LAG_TRANSPOSE):
                xhat_t = transpose_group(i - LAG_TRANSPOSE)
            if 0 <= i - 1 < N_WEIGHTS:
                transpose_weight(i - 1)
            if in_range(i - LAG_SCALARS):
                std = standard_deviation(i - LAG_SCALARS)
                negate_mean(i - LAG_SCALARS)
            if in_range(i - LAG_NORMALISE):
                normalise(i - LAG_NORMALISE)
            if in_range(i - LAG_TRANSPOSE):
                gain_shift_group(i - LAG_TRANSPOSE, xhat_t)
            if in_range(i):
                statistics(i)
            if in_range(i - LAG_SCALARS):
                invert(i - LAG_SCALARS, std)
            if 0 <= i - 1 < N_WEIGHTS:
                quantise_weight(i - 1)
            if in_range(i - LAG_PROJECT):
                project_group(i - LAG_PROJECT, codes, scales)
